import numpy as np
import ml_dtypes


def mxq(x, axis, fmt="e4m3"):
    dtype, down = {"e4m3": (ml_dtypes.float8_e4m3fn, 7), "e5m2": (ml_dtypes.float8_e5m2, 14)}[fmt]
    v = np.moveaxis(np.asarray(x, np.float32).astype(ml_dtypes.bfloat16).astype(np.float64), axis, -1)
    blocks = v.reshape(v.shape[:-1] + (-1, 32))
    amax = np.abs(blocks).max(-1, keepdims=True)
    byte = np.maximum(np.where(amax > 0, np.frexp(amax)[1] - 1 + 127, 0) - down, 1)
    scale = np.exp2(byte - 127.0)
    codes = (blocks / scale).astype(np.float32).astype(dtype).astype(np.float64)
    return np.moveaxis((codes * scale).reshape(v.shape), -1, axis)


WIDE = False


def mx_kscale(k):
    if not WIDE:
        return np.ones(k)
    levels = np.array([30, -30])
    if k % 512:
        return np.exp2(np.random.permutation(np.resize(levels, k // 32))).repeat(32)
    a = np.empty((k // 512, 16))
    for p in range(k // 512):
        a[p, :8] = np.random.permutation(np.resize(levels, 8))
        for g in range(8):
            far = levels[np.abs(levels - a[p, g]) >= 10]
            a[p, g + 8] = far[np.random.randint(len(far))]
    return np.exp2(a.ravel()).repeat(32)


BF16 = ml_dtypes.bfloat16


def bf(x):
    return np.asarray(x, np.float32).astype(BF16)


def f64(x):
    return np.asarray(x).astype(np.float64)


B, S, H, N_HEADS, N_KV, D, QB, ORIG_MAX_POS = 1, 1024, 2048, 16, 4, 128, 512, 8192
ROPE_BASE = 5.0e5
ROPE_FACTOR = 8.0
LOW_FREQ, HIGH_FREQ = 1.0, 4.0


def llama3_cos_sin():
    inv_freq = 1.0 / (ROPE_BASE ** (np.arange(0, D, 2) / D))
    wavelen = 2.0 * np.pi / inv_freq
    smooth = np.clip((ORIG_MAX_POS / wavelen - LOW_FREQ) / (HIGH_FREQ - LOW_FREQ), 0.0, 1.0)
    new_inv_freq = (1.0 - smooth) * (inv_freq / ROPE_FACTOR) + smooth * inv_freq
    freqs = np.arange(S)[:, None] * new_inv_freq[None, :]
    emb = np.concatenate([freqs, freqs], axis=-1)
    return np.cos(emb), np.sin(emb)


def rotate_half(x):
    x1, x2 = x[..., : D // 2], x[..., D // 2:]
    return np.concatenate([-x2, x1], axis=-1)


def apply_rope(x, cos, sin):
    return x * cos[None, None, :, :] + rotate_half(x) * sin[None, None, :, :]


def setup_inputs():
    s = mx_kscale(H)
    return {"hidden_states": bf(np.random.standard_normal((B, S, H)) * s),
            "wq": bf(np.random.standard_normal((N_HEADS * D, H)) / np.sqrt(H) / s[None, :]),
            "wk": bf(np.random.standard_normal((N_KV * D, H)) / np.sqrt(H) / s[None, :])}


def reference(hidden_states, wq, wk):
    xq = mxq(f64(hidden_states), 2, "e5m2")
    q = (xq @ mxq(f64(wq), 1, "e5m2").T).reshape(B, S, N_HEADS, D).transpose(0, 2, 1, 3)
    k = (xq @ mxq(f64(wk), 1, "e5m2").T).reshape(B, S, N_KV, D).transpose(0, 2, 1, 3)
    cos, sin = llama3_cos_sin()
    return apply_rope(q, cos, sin), apply_rope(k, cos, sin)

@@ -1,0 +1,276 @@
+from contextlib import ExitStack
+
+import concourse.mybir as mybir
+from concourse.masks import make_identity
+
+S, K, D = 1024, 2048, 128
+Q_HEADS, KV_HEADS = 16, 4
+ROPE_BASE, ROPE_FACTOR, ORIG_MAX_POS = 5.0e5, 8.0, 8192
+LOW_FREQ, HIGH_FREQ = 1.0, 4.0
+
+FLOPS = 2 * S * (Q_HEADS + KV_HEADS) * D * K
+
+F32 = mybir.dt.float32
+BF16 = mybir.dt.bfloat16
+I32 = mybir.dt.int32
+U32 = mybir.dt.uint32
+U8 = mybir.dt.uint8
+E5M2X4 = mybir.dt.float8_e5m2_x4
+ALU = mybir.AluOpType
+ACT = mybir.ActivationFunctionType
+
+PI = 3.141592653589793
+P = 128
+HALF = D // 2
+PASSES = K // 512
+TOKEN_TILES = S // P
+GROUP_HEADS = 4
+GROUPS = (Q_HEADS + KV_HEADS) // GROUP_HEADS
+RAW_BUFS = 14
+
+HEAD_UNITS = 6
+UNITS_AFTER_FIRST_GROUP = (2, 2, 2, 2, 1, 1, 0, 0)
+UNITS_AFTER_LATER_GROUP = (0, 2, 0, 0, 2, 0, 0, 0)
+
+TWO_PI_HI = 6.28125
+TWO_PI_LO = 2.0 * PI - TWO_PI_HI
+
+
+def rope_smooth(j):
+    inv_freq = ROPE_BASE ** (-2.0 * j / D)
+    ratio = ORIG_MAX_POS * inv_freq / (2.0 * PI)
+    return min(max((ratio - LOW_FREQ) / (HIGH_FREQ - LOW_FREQ), 0.0), 1.0)
+
+
+def rope_freq(j):
+    inv_freq = ROPE_BASE ** (-2.0 * j / D)
+    smooth = rope_smooth(j)
+    return (1.0 - smooth) * inv_freq / ROPE_FACTOR + smooth * inv_freq
+
+
+def build_rope_tables(nc, keep, work):
+    width = TOKEN_TILES * HALF
+    tpos = work.tile([P, TOKEN_TILES, 1], F32, name="tpos")
+    nc.gpsimd.iota(
+        tpos[:].rearrange("p t o -> p (t o)"),
+        pattern=[[1, TOKEN_TILES]],
+        base=0,
+        channel_multiplier=TOKEN_TILES,
+        allow_small_or_imprecise_dtypes=True,
+    )
+
+    angle = work.tile([P, TOKEN_TILES, HALF], F32, name="angle")
+    nc.vector.tensor_copy(out=angle[:, :, 0:1], in_=tpos[:])
+    for level in range(6):
+        w = 2**level
+        nc.vector.tensor_scalar(
+            out=angle[:, :, w : 2 * w],
+            in0=angle[:, :, 0:w],
+            scalar1=ROPE_BASE ** (-2.0 * w / D),
+            scalar2=None,
+            op0=ALU.mult,
+        )
+    divided = [j for j in range(HALF) if rope_smooth(j) == 0.0]
+    assert divided == list(range(divided[0], HALF))
+    nc.vector.tensor_scalar(
+        out=angle[:, :, divided[0] :],
+        in0=angle[:, :, divided[0] :],
+        scalar1=1.0 / ROPE_FACTOR,
+        scalar2=None,
+        op0=ALU.mult,
+    )
+    for j in range(HALF):
+        if 0.0 < rope_smooth(j) < 1.0:
+            nc.vector.tensor_scalar(
+                out=angle[:, :, j : j + 1], in0=tpos[:], scalar1=rope_freq(j), scalar2=None, op0=ALU.mult
+            )
+    angle_flat = angle[:].rearrange("p t j -> p (t j)")
+
+    turns_int = work.tile([P, width], I32, name="turns_int")
+    nc.vector.tensor_scalar(
+        out=turns_int[:], in0=angle_flat, scalar1=1.0 / (2.0 * PI), scalar2=0.25, op0=ALU.mult, op1=ALU.add
+    )
+    turns = work.tile([P, width], F32, name="turns")
+    nc.vector.tensor_copy(out=turns[:], in_=turns_int[:])
+    rest_hi = work.tile([P, width], F32, name="rest_hi")
+    nc.vector.scalar_tensor_tensor(
+        out=rest_hi[:], in0=turns[:], scalar=-TWO_PI_HI, in1=angle_flat, op0=ALU.mult, op1=ALU.add
+    )
+    rest = work.tile([P, width], F32, name="rest")
+    nc.vector.scalar_tensor_tensor(
+        out=rest[:], in0=turns[:], scalar=-TWO_PI_LO, in1=rest_hi[:], op0=ALU.mult, op1=ALU.add
+    )
+
+    sin_half = work.tile([P, TOKEN_TILES, HALF], F32, name="sin_half")
+    nc.scalar.activation(out=sin_half[:].rearrange("p t j -> p (t j)"), in_=rest[:], func=ACT.Sin, scale=0.5)
+    sin_quarter = work.tile([P, TOKEN_TILES, HALF], F32, name="sin_quarter")
+    nc.scalar.activation(out=sin_quarter[:].rearrange("p t j -> p (t j)"), in_=rest[:], func=ACT.Sin, scale=0.25)
+
+    cos2 = keep.tile([P, TOKEN_TILES, D], F32, name="cos2")
+    sin2 = keep.tile([P, TOKEN_TILES, D], F32, name="sin2")
+    square_half = work.tile([P, TOKEN_TILES, HALF], F32, name="square_half")
+    nc.vector.tensor_tensor(out=square_half[:], in0=sin_half[:], in1=sin_half[:], op=ALU.mult)
+    for lo in (0, HALF):
+        nc.vector.tensor_scalar(
+            out=cos2[:, :, lo : lo + HALF], in0=square_half[:], scalar1=-2.0, scalar2=1.0, op0=ALU.mult, op1=ALU.add
+        )
+    two_cos_half = work.tile([P, TOKEN_TILES, HALF], F32, name="two_cos_half")
+    nc.gpsimd.tensor_tensor(out=two_cos_half[:], in0=sin_quarter[:], in1=sin_quarter[:], op=ALU.mult)
+    nc.gpsimd.tensor_scalar(
+        out=two_cos_half[:], in0=two_cos_half[:], scalar1=-4.0, scalar2=2.0, op0=ALU.mult, op1=ALU.add
+    )
+    nc.gpsimd.tensor_tensor(out=sin2[:, :, 0:HALF], in0=sin_half[:], in1=two_cos_half[:], op=ALU.mult)
+    nc.gpsimd.tensor_scalar(
+        out=sin2[:, :, HALF:D], in0=sin2[:, :, 0:HALF], scalar1=-1.0, scalar2=0.0, op0=ALU.mult, op1=ALU.add
+    )
+    return cos2, sin2
+
+
+def tile_stickyllamaattention_pa_kernel(tc, hidden_states, wq, wk, out_0, out_1):
+    nc = tc.nc
+
+    x_rows = hidden_states[0].rearrange("(p e) k -> e p k", e=TOKEN_TILES)
+    units = [("w", 0, h) for h in range(GROUP_HEADS)]
+    units += [("x", t, 0) for t in range(TOKEN_TILES)]
+    units += [("w", n, h) for n in range(1, GROUPS) for h in range(GROUP_HEADS)]
+
+    def unit_rows(unit):
+        kind, a, b = unit
+        if kind == "x":
+            return x_rows[a]
+        head = GROUP_HEADS * a + b
+        if head < Q_HEADS:
+            return wq[head * D : (head + 1) * D, :]
+        return wk[(head - Q_HEADS) * D : (head - Q_HEADS + 1) * D, :]
+
+    q_view = out_0[0].rearrange("h (p e) d -> p h (e d)", e=TOKEN_TILES)
+    k_view = out_1[0].rearrange("h (p e) d -> p h (e d)", e=TOKEN_TILES)
+
+    with ExitStack() as ctx:
+        keep = ctx.enter_context(tc.tile_pool(name="keep", bufs=1))
+        work = ctx.enter_context(tc.tile_pool(name="work", bufs=1))
+        raw_pool = ctx.enter_context(tc.tile_pool(name="raw", bufs=RAW_BUFS))
+        x_stage = ctx.enter_context(tc.tile_pool(name="x_stage", bufs=3))
+        w_stage = ctx.enter_context(tc.tile_pool(name="w_stage", bufs=2))
+        rope_pool = ctx.enter_context(tc.tile_pool(name="rope", bufs=3))
+        turn_psum = ctx.enter_context(tc.psum_pool(name="turn_psum", bufs=4))
+        acc_psum = ctx.enter_context(tc.psum_pool(name="acc_psum", bufs=4))
+
+        raw_tiles = {}
+
+        def load(i):
+            if i < len(units):
+                raw = raw_pool.tile([P, K], BF16, name="raw")
+                nc.sync.dma_start(out=raw[:], in_=unit_rows(units[i]))
+                raw_tiles[i] = raw
+
+        for i in range(RAW_BUFS):
+            load(i)
+
+        zero = work.tile([P, 1], F32, name="zero")
+        nc.vector.memset(zero[:], 0.0)
+        warm = work.tile([P, 1], F32, name="warm")
+        nc.scalar.activation(out=warm[:], in_=zero[:], func=ACT.Sin)
+
+        ident = keep.tile([P, P], F32, name="ident")
+        make_identity(nc, ident[:])
+        cos2, sin2 = build_rope_tables(nc, keep, work)
+
+        x_codes = [keep.tile([P, PASSES, P], U32, name="x_codes%d" % t, align_bytes=64) for t in range(TOKEN_TILES)]
+        x_scales = [keep.tile([P, PASSES, P], U8, name="x_scales%d" % t, align_bytes=64) for t in range(TOKEN_TILES)]
+        w_codes = [keep.tile([P, PASSES, 512], U32, name="w_codes%d" % n, align_bytes=64) for n in range(GROUPS)]
+        w_scales = [keep.tile([P, PASSES, 512], U8, name="w_scales%d" % n, align_bytes=64) for n in range(GROUPS)]
+        w_grouped = {}
+
+        def prepare(i):
+            kind, a, b = units[i]
+            words = raw_tiles[i][:].bitcast(F32)
+            if kind == "x":
+                grouped = x_stage.tile([P, PASSES, 4 * P], BF16, name="x_grouped", align_bytes=64)
+                dest = grouped[:].bitcast(F32).rearrange("p g (r u) -> p g r u", u=2)
+            else:
+                if b == 0:
+                    w_grouped[a] = w_stage.tile([P, PASSES, 4 * 512], BF16, name="w_grouped", align_bytes=64)
+                grouped = w_grouped[a]
+                dest = grouped[:].bitcast(F32).rearrange("p g (h r u) -> p g h r u", h=GROUP_HEADS, u=2)[:, :, b]
+            for bank in range(PASSES // 2):
+                turned = turn_psum.tile([P, 4, P], F32, name="turned")
+                for slot in range(4):
+                    g, u = 2 * bank + slot // 2, slot % 2
+                    nc.tensor.transpose(
+                        out=turned[:, slot, :], in_=words[:, 256 * g + u : 256 * (g + 1) : 2], identity=ident[:]
+                    )
+                nc.scalar.copy(
+                    out=dest[:, 2 * bank : 2 * bank + 2],
+                    in_=turned[:].rearrange("p (g u) r -> p g r u", u=2),
+                )
+            if kind == "x":
+                nc.vector.quantize_mx(
+                    out=x_codes[a][:].rearrange("p g r -> p (g r)").bitcast(E5M2X4),
+                    scales=x_scales[a][:].rearrange("p g r -> p (g r)"),
+                    in_=grouped[:].rearrange("p g c -> p (g c)"),
+                )
+            elif b == GROUP_HEADS - 1:
+                for g in range(PASSES):
+                    nc.vector.quantize_mx(
+                        out=w_codes[a][:, g, :].bitcast(E5M2X4), scales=w_scales[a][:, g, :], in_=grouped[:, g, :]
+                    )
+            load(i + RAW_BUFS)
+
+        pair = {}
+
+        def product(n, t):
+            acc = acc_psum.tile([P, GROUP_HEADS, D], F32, name="acc")
+            for g in range(PASSES):
+                nc.tensor.matmul_mx(
+                    out=acc[:].rearrange("p h d -> p (h d)"),
+                    lhsT=x_codes[t][:, g, :].bitcast(E5M2X4),
+                    lhsT_scale=x_scales[t][:, g, :],
+                    rhs=w_codes[n][:, g, :].bitcast(E5M2X4),
+                    rhs_scale=w_scales[n][:, g, :],
+                    start=(g == 0),
+                    stop=(g == PASSES - 1),
+                )
+            e = t % 2
+            if e == 0:
+                pair["by_cos"] = rope_pool.tile([P, GROUP_HEADS, 2, D], F32, name="by_cos")
+                pair["by_sin"] = rope_pool.tile([P, GROUP_HEADS, 2, D], F32, name="by_sin")
+            by_cos, by_sin = pair["by_cos"], pair["by_sin"]
+            nc.vector.tensor_tensor(
+                out=by_cos[:, :, e, :],
+                in0=acc[:],
+                in1=cos2[:, t, :].unsqueeze(1).to_broadcast([P, GROUP_HEADS, D]),
+                op=ALU.mult,
+            )
+            nc.vector.tensor_tensor(
+                out=by_sin[:, :, e, :],
+                in0=acc[:],
+                in1=sin2[:, t, :].unsqueeze(1).to_broadcast([P, GROUP_HEADS, D]),
+                op=ALU.mult,
+            )
+            if e == 1:
+                rows_cos = by_cos[:].rearrange("p h e d -> p (h e) d")
+                rows_sin = by_sin[:].rearrange("p h e d -> p (h e) d")
+                for lo in (0, HALF):
+                    nc.gpsimd.tensor_tensor(
+                        out=rows_cos[:, :, lo : lo + HALF],
+                        in0=rows_cos[:, :, lo : lo + HALF],
+                        in1=rows_sin[:, :, HALF - lo : D - lo],
+                        op=ALU.add,
+                    )
+                view = q_view[:, GROUP_HEADS * n : GROUP_HEADS * (n + 1)] if n < GROUPS - 1 else k_view
+                nc.sync.dma_start(
+                    out=view[:, :, (t - 1) * D : (t + 1) * D], in_=by_cos[:].rearrange("p h e d -> p h (e d)")
+                )
+
+        with tc.manual_schedule(engines={mybir.EngineType.PE}):
+            for i in range(HEAD_UNITS):
+                prepare(i)
+            done = HEAD_UNITS
+            for n in range(GROUPS):
+                after = UNITS_AFTER_FIRST_GROUP if n == 0 else UNITS_AFTER_LATER_GROUP
+                for t in range(TOKEN_TILES):
+                    product(n, t)
+                    for i in range(done, min(done + after[t], len(units))):
+                        prepare(i)
+                    done = min(done + after[t], len(units))

@@ -26,11 +26,17 @@ PASSES = K // 512
 TOKEN_TILES = S // P
 GROUP_HEADS = 4
 GROUPS = (Q_HEADS + KV_HEADS) // GROUP_HEADS
-RAW_BUFS = 14
+RAW_BUFS = 12
 
 HEAD_UNITS = 6
-UNITS_AFTER_FIRST_GROUP = (2, 2, 2, 2, 1, 1, 0, 0)
-UNITS_AFTER_LATER_GROUP = (0, 2, 0, 0, 2, 0, 0, 0)
+EARLY_UNITS = 16
+LATE_FIRST_PRODUCT = 7
+LINE_AHEAD = 2
+
+
+def lined_up(i):
+    return i >= EARLY_UNITS
+
 
 TWO_PI_HI = 6.28125
 TWO_PI_LO = 2.0 * PI - TWO_PI_HI
@@ -48,8 +54,15 @@ def rope_freq(j):
     return (1.0 - smooth) * inv_freq / ROPE_FACTOR + smooth * inv_freq
 
 
-def build_rope_tables(nc, keep, work):
-    width = TOKEN_TILES * HALF
+def scratch(work, slot, name, dtype=F32):
+    return work.tile([P, TOKEN_TILES, HALF], dtype, name=name, tag="scratch_" + slot)
+
+
+def flat(tile_ap):
+    return tile_ap[:].rearrange("p t j -> p (t j)")
+
+
+def reduced_angles(nc, work):
     tpos = work.tile([P, TOKEN_TILES, 1], F32, name="tpos")
     nc.gpsimd.iota(
         tpos[:].rearrange("p t o -> p (t o)"),
@@ -59,7 +72,7 @@ def build_rope_tables(nc, keep, work):
         allow_small_or_imprecise_dtypes=True,
     )
 
-    angle = work.tile([P, TOKEN_TILES, HALF], F32, name="angle")
+    angle = scratch(work, "a", "angle")
     nc.vector.tensor_copy(out=angle[:, :, 0:1], in_=tpos[:])
     for level in range(6):
         w = 2**level
@@ -84,46 +97,52 @@ def build_rope_tables(nc, keep, work):
             nc.vector.tensor_scalar(
                 out=angle[:, :, j : j + 1], in0=tpos[:], scalar1=rope_freq(j), scalar2=None, op0=ALU.mult
             )
-    angle_flat = angle[:].rearrange("p t j -> p (t j)")
 
-    turns_int = work.tile([P, width], I32, name="turns_int")
+    turns_int = scratch(work, "b", "turns_int", I32)
     nc.vector.tensor_scalar(
-        out=turns_int[:], in0=angle_flat, scalar1=1.0 / (2.0 * PI), scalar2=0.25, op0=ALU.mult, op1=ALU.add
+        out=flat(turns_int), in0=flat(angle), scalar1=1.0 / (2.0 * PI), scalar2=0.25, op0=ALU.mult, op1=ALU.add
     )
-    turns = work.tile([P, width], F32, name="turns")
-    nc.vector.tensor_copy(out=turns[:], in_=turns_int[:])
-    rest_hi = work.tile([P, width], F32, name="rest_hi")
+    turns = scratch(work, "c", "turns")
+    nc.vector.tensor_copy(out=flat(turns), in_=flat(turns_int))
+    rest_hi = scratch(work, "d", "rest_hi")
     nc.vector.scalar_tensor_tensor(
-        out=rest_hi[:], in0=turns[:], scalar=-TWO_PI_HI, in1=angle_flat, op0=ALU.mult, op1=ALU.add
+        out=flat(rest_hi), in0=flat(turns), scalar=-TWO_PI_HI, in1=flat(angle), op0=ALU.mult, op1=ALU.add
     )
-    rest = work.tile([P, width], F32, name="rest")
+    rest = scratch(work, "a", "rest")
     nc.vector.scalar_tensor_tensor(
-        out=rest[:], in0=turns[:], scalar=-TWO_PI_LO, in1=rest_hi[:], op0=ALU.mult, op1=ALU.add
+        out=flat(rest), in0=flat(turns), scalar=-TWO_PI_LO, in1=flat(rest_hi), op0=ALU.mult, op1=ALU.add
     )
+    return rest
 
-    sin_half = work.tile([P, TOKEN_TILES, HALF], F32, name="sin_half")
-    nc.scalar.activation(out=sin_half[:].rearrange("p t j -> p (t j)"), in_=rest[:], func=ACT.Sin, scale=0.5)
-    sin_quarter = work.tile([P, TOKEN_TILES, HALF], F32, name="sin_quarter")
-    nc.scalar.activation(out=sin_quarter[:].rearrange("p t j -> p (t j)"), in_=rest[:], func=ACT.Sin, scale=0.25)
 
-    cos2 = keep.tile([P, TOKEN_TILES, D], F32, name="cos2")
-    sin2 = keep.tile([P, TOKEN_TILES, D], F32, name="sin2")
-    square_half = work.tile([P, TOKEN_TILES, HALF], F32, name="square_half")
+def rope_tables(nc, keep, work, rest):
+    sin_half = scratch(work, "b", "sin_half")
+    nc.scalar.activation(out=flat(sin_half), in_=flat(rest), func=ACT.Sin, scale=0.5)
+    sin_quarter = scratch(work, "c", "sin_quarter")
+    nc.scalar.activation(out=flat(sin_quarter), in_=flat(rest), func=ACT.Sin, scale=0.25)
+
+    cos_sin = keep.tile([P, TOKEN_TILES, 2, D], F32, name="cos_sin")
+    square_half = scratch(work, "d", "square_half")
     nc.vector.tensor_tensor(out=square_half[:], in0=sin_half[:], in1=sin_half[:], op=ALU.mult)
     for lo in (0, HALF):
         nc.vector.tensor_scalar(
-            out=cos2[:, :, lo : lo + HALF], in0=square_half[:], scalar1=-2.0, scalar2=1.0, op0=ALU.mult, op1=ALU.add
+            out=cos_sin[:, :, 0, lo : lo + HALF],
+            in0=square_half[:],
+            scalar1=-2.0,
+            scalar2=1.0,
+            op0=ALU.mult,
+            op1=ALU.add,
         )
-    two_cos_half = work.tile([P, TOKEN_TILES, HALF], F32, name="two_cos_half")
+    two_cos_half = scratch(work, "a", "two_cos_half")
     nc.gpsimd.tensor_tensor(out=two_cos_half[:], in0=sin_quarter[:], in1=sin_quarter[:], op=ALU.mult)
     nc.gpsimd.tensor_scalar(
         out=two_cos_half[:], in0=two_cos_half[:], scalar1=-4.0, scalar2=2.0, op0=ALU.mult, op1=ALU.add
     )
-    nc.gpsimd.tensor_tensor(out=sin2[:, :, 0:HALF], in0=sin_half[:], in1=two_cos_half[:], op=ALU.mult)
+    nc.gpsimd.tensor_tensor(out=cos_sin[:, :, 1, 0:HALF], in0=sin_half[:], in1=two_cos_half[:], op=ALU.mult)
     nc.gpsimd.tensor_scalar(
-        out=sin2[:, :, HALF:D], in0=sin2[:, :, 0:HALF], scalar1=-1.0, scalar2=0.0, op0=ALU.mult, op1=ALU.add
+        out=cos_sin[:, :, 1, HALF:D], in0=cos_sin[:, :, 1, 0:HALF], scalar1=-1.0, scalar2=0.0, op0=ALU.mult, op1=ALU.add
     )
-    return cos2, sin2
+    return cos_sin
 
 
 def tile_stickyllamaattention_pa_kernel(tc, hidden_states, wq, wk, out_0, out_1):
@@ -152,9 +171,11 @@ def tile_stickyllamaattention_pa_kernel(tc, hidden_states, wq, wk, out_0, out_1)
         raw_pool = ctx.enter_context(tc.tile_pool(name="raw", bufs=RAW_BUFS))
         x_stage = ctx.enter_context(tc.tile_pool(name="x_stage", bufs=3))
         w_stage = ctx.enter_context(tc.tile_pool(name="w_stage", bufs=2))
+        line_pool = ctx.enter_context(tc.tile_pool(name="line", bufs=4))
         rope_pool = ctx.enter_context(tc.tile_pool(name="rope", bufs=3))
         turn_psum = ctx.enter_context(tc.psum_pool(name="turn_psum", bufs=4))
         acc_psum = ctx.enter_context(tc.psum_pool(name="acc_psum", bufs=4))
+        ctx.enter_context(tc.manual_schedule())
 
         raw_tiles = {}
 
@@ -172,15 +193,24 @@ def tile_stickyllamaattention_pa_kernel(tc, hidden_states, wq, wk, out_0, out_1)
         warm = work.tile([P, 1], F32, name="warm")
         nc.scalar.activation(out=warm[:], in_=zero[:], func=ACT.Sin)
 
+        rest = reduced_angles(nc, work)
         ident = keep.tile([P, P], F32, name="ident")
         make_identity(nc, ident[:])
-        cos2, sin2 = build_rope_tables(nc, keep, work)
 
         x_codes = [keep.tile([P, PASSES, P], U32, name="x_codes%d" % t, align_bytes=64) for t in range(TOKEN_TILES)]
         x_scales = [keep.tile([P, PASSES, P], U8, name="x_scales%d" % t, align_bytes=64) for t in range(TOKEN_TILES)]
         w_codes = [keep.tile([P, PASSES, 512], U32, name="w_codes%d" % n, align_bytes=64) for n in range(GROUPS)]
         w_scales = [keep.tile([P, PASSES, 512], U8, name="w_scales%d" % n, align_bytes=64) for n in range(GROUPS)]
         w_grouped = {}
+        lined_tiles = {}
+
+        def line_up(i):
+            if i < len(units) and lined_up(i):
+                lined = line_pool.tile([P, PASSES, 2, P], F32, name="lined")
+                nc.scalar.copy(
+                    out=lined[:], in_=raw_tiles[i][:].bitcast(F32).rearrange("p (g w u) -> p g u w", g=PASSES, u=2)
+                )
+                lined_tiles[i] = lined
 
         def prepare(i):
             kind, a, b = units[i]
@@ -197,9 +227,8 @@ def tile_stickyllamaattention_pa_kernel(tc, hidden_states, wq, wk, out_0, out_1)
                 turned = turn_psum.tile([P, 4, P], F32, name="turned")
                 for slot in range(4):
                     g, u = 2 * bank + slot // 2, slot % 2
-                    nc.tensor.transpose(
-                        out=turned[:, slot, :], in_=words[:, 256 * g + u : 256 * (g + 1) : 2], identity=ident[:]
-                    )
+                    source = lined_tiles[i][:, g, u, :] if lined_up(i) else words[:, 256 * g + u : 256 * (g + 1) : 2]
+                    nc.tensor.transpose(out=turned[:, slot, :], in_=source, identity=ident[:])
                 nc.scalar.copy(
                     out=dest[:, 2 * bank : 2 * bank + 2],
                     in_=turned[:].rearrange("p (g u) r -> p g r u", u=2),
@@ -211,11 +240,20 @@ def tile_stickyllamaattention_pa_kernel(tc, hidden_states, wq, wk, out_0, out_1)
                     in_=grouped[:].rearrange("p g c -> p (g c)"),
                 )
             elif b == GROUP_HEADS - 1:
-                for g in range(PASSES):
+                for g in range(0, PASSES, 2):
                     nc.vector.quantize_mx(
-                        out=w_codes[a][:, g, :].bitcast(E5M2X4), scales=w_scales[a][:, g, :], in_=grouped[:, g, :]
+                        out=w_codes[a][:, g : g + 2, :].rearrange("p g c -> p (g c)").bitcast(E5M2X4),
+                        scales=w_scales[a][:, g : g + 2, :].rearrange("p g c -> p (g c)"),
+                        in_=grouped[:, g : g + 2, :].rearrange("p g c -> p (g c)"),
                     )
             load(i + RAW_BUFS)
+
+        def prepare_run(first, count):
+            for i in range(first, first + count):
+                prepare(i)
+            for i in range(first + count, first + count + LINE_AHEAD):
+                if i not in lined_tiles:
+                    line_up(i)
 
         pair = {}
 
@@ -233,44 +271,44 @@ def tile_stickyllamaattention_pa_kernel(tc, hidden_states, wq, wk, out_0, out_1)
                 )
             e = t % 2
             if e == 0:
-                pair["by_cos"] = rope_pool.tile([P, GROUP_HEADS, 2, D], F32, name="by_cos")
-                pair["by_sin"] = rope_pool.tile([P, GROUP_HEADS, 2, D], F32, name="by_sin")
-            by_cos, by_sin = pair["by_cos"], pair["by_sin"]
+                pair["prod"] = rope_pool.tile([P, 2, GROUP_HEADS, 2, D], F32, name="prod")
+            prod = pair["prod"]
             nc.vector.tensor_tensor(
-                out=by_cos[:, :, e, :],
-                in0=acc[:],
-                in1=cos2[:, t, :].unsqueeze(1).to_broadcast([P, GROUP_HEADS, D]),
+                out=prod[:, :, :, e, :],
+                in0=acc[:].unsqueeze(1).to_broadcast([P, 2, GROUP_HEADS, D]),
+                in1=tables["cos_sin"][:, t].unsqueeze(2).to_broadcast([P, 2, GROUP_HEADS, D]),
                 op=ALU.mult,
             )
-            nc.vector.tensor_tensor(
-                out=by_sin[:, :, e, :],
-                in0=acc[:],
-                in1=sin2[:, t, :].unsqueeze(1).to_broadcast([P, GROUP_HEADS, D]),
-                op=ALU.mult,
-            )
-            if e == 1:
-                rows_cos = by_cos[:].rearrange("p h e d -> p (h e) d")
-                rows_sin = by_sin[:].rearrange("p h e d -> p (h e) d")
+            view = q_view[:, GROUP_HEADS * n : GROUP_HEADS * (n + 1)] if n < GROUPS - 1 else k_view
+            if n == GROUPS - 1 and t >= TOKEN_TILES - 2:
                 for lo in (0, HALF):
-                    nc.gpsimd.tensor_tensor(
-                        out=rows_cos[:, :, lo : lo + HALF],
-                        in0=rows_cos[:, :, lo : lo + HALF],
-                        in1=rows_sin[:, :, HALF - lo : D - lo],
+                    nc.vector.tensor_tensor(
+                        out=prod[:, 0, :, e, lo : lo + HALF],
+                        in0=prod[:, 0, :, e, lo : lo + HALF],
+                        in1=prod[:, 1, :, e, HALF - lo : D - lo],
                         op=ALU.add,
                     )
-                view = q_view[:, GROUP_HEADS * n : GROUP_HEADS * (n + 1)] if n < GROUPS - 1 else k_view
+                nc.scalar.dma_start(out=view[:, :, t * D : (t + 1) * D], in_=prod[:, 0, :, e, :])
+            elif e == 1:
+                by_cos = prod[:, 0].rearrange("p h e (a j) -> p (h e) a j", a=2)
+                by_sin = prod[:, 1].rearrange("p h e (a j) -> p (h e) a j", a=2)
+                nc.gpsimd.tensor_tensor(out=by_cos, in0=by_cos, in1=by_sin[:, :, ::-1, :], op=ALU.add)
                 nc.sync.dma_start(
-                    out=view[:, :, (t - 1) * D : (t + 1) * D], in_=by_cos[:].rearrange("p h e d -> p h (e d)")
+                    out=view[:, :, (t - 1) * D : (t + 1) * D], in_=prod[:, 0].rearrange("p h e d -> p h (e d)")
                 )
 
-        with tc.manual_schedule(engines={mybir.EngineType.PE}):
-            for i in range(HEAD_UNITS):
-                prepare(i)
-            done = HEAD_UNITS
-            for n in range(GROUPS):
-                after = UNITS_AFTER_FIRST_GROUP if n == 0 else UNITS_AFTER_LATER_GROUP
-                for t in range(TOKEN_TILES):
-                    product(n, t)
-                    for i in range(done, min(done + after[t], len(units))):
-                        prepare(i)
-                    done = min(done + after[t], len(units))
+        tables = {}
+        prepare_run(0, 2)
+        tables["cos_sin"] = rope_tables(nc, keep, work, rest)
+        prepare_run(2, HEAD_UNITS - 2)
+        done = HEAD_UNITS
+        for number in range(GROUPS * TOKEN_TILES):
+            product(number // TOKEN_TILES, number % TOKEN_TILES)
+            if done < EARLY_UNITS:
+                count = 2
+            elif done < len(units) and number >= LATE_FIRST_PRODUCT and (number - LATE_FIRST_PRODUCT) % 2 == 0:
+                count = 1
+            else:
+                count = 0
+            prepare_run(done, count)
+            done += count

@@ -31,6 +31,8 @@ RAW_BUFS = 12
 HEAD_UNITS = 6
 EARLY_UNITS = 16
 LATE_FIRST_PRODUCT = 7
+WARM_UP = 8
+KEEP_WARM = 2
 LINE_AHEAD = 2
 
 
@@ -188,6 +190,18 @@ def tile_stickyllamaattention_pa_kernel(tc, hidden_states, wq, wk, out_0, out_1)
         for i in range(RAW_BUFS):
             load(i)
 
+        idle = keep.tile([P, 512], BF16, name="idle")
+        nc.gpsimd.memset(idle[:], 0.0)
+        spin = acc_psum.tile([P, GROUP_HEADS, D], F32, name="acc")
+
+        def idle_matmuls(count):
+            for k in range(count):
+                nc.tensor.matmul(
+                    out=spin[:].rearrange("p h d -> p (h d)"), lhsT=idle[:, 0:P], rhs=idle[:], start=True, stop=True
+                )
+
+        idle_matmuls(WARM_UP)
+
         zero = work.tile([P, 1], F32, name="zero")
         nc.vector.memset(zero[:], 0.0)
         warm = work.tile([P, 1], F32, name="warm")
@@ -251,6 +265,8 @@ def tile_stickyllamaattention_pa_kernel(tc, hidden_states, wq, wk, out_0, out_1)
         def prepare_run(first, count):
             for i in range(first, first + count):
                 prepare(i)
+                if i < HEAD_UNITS:
+                    idle_matmuls(KEEP_WARM)
             for i in range(first + count, first + count + LINE_AHEAD):
                 if i not in lined_tiles:
                     line_up(i)

@@ -33,7 +33,7 @@ EARLY_UNITS = 16
 LATE_FIRST_PRODUCT = 7
 WARM_UP = 8
 KEEP_WARM = 2
-LINE_AHEAD = 2
+LINE_AHEAD = 4
 
 
 def lined_up(i):
@@ -153,7 +153,8 @@ def tile_stickyllamaattention_pa_kernel(tc, hidden_states, wq, wk, out_0, out_1)
     x_rows = hidden_states[0].rearrange("(p e) k -> e p k", e=TOKEN_TILES)
     units = [("w", 0, h) for h in range(GROUP_HEADS)]
     units += [("x", t, 0) for t in range(TOKEN_TILES)]
-    units += [("w", n, h) for n in range(1, GROUPS) for h in range(GROUP_HEADS)]
+    units += [("w", 1, h) for h in range(GROUP_HEADS)]
+    units += [("g", n, b) for n in range(2, GROUPS) for b in range(GROUP_HEADS)]
 
     def unit_rows(unit):
         kind, a, b = unit
@@ -171,9 +172,9 @@ def tile_stickyllamaattention_pa_kernel(tc, hidden_states, wq, wk, out_0, out_1)
         keep = ctx.enter_context(tc.tile_pool(name="keep", bufs=1))
         work = ctx.enter_context(tc.tile_pool(name="work", bufs=1))
         raw_pool = ctx.enter_context(tc.tile_pool(name="raw", bufs=RAW_BUFS))
-        x_stage = ctx.enter_context(tc.tile_pool(name="x_stage", bufs=3))
-        w_stage = ctx.enter_context(tc.tile_pool(name="w_stage", bufs=2))
-        line_pool = ctx.enter_context(tc.tile_pool(name="line", bufs=4))
+        stage = ctx.enter_context(tc.tile_pool(name="stage", bufs=3))
+        w_stage = ctx.enter_context(tc.tile_pool(name="w_stage", bufs=1))
+        line_pool = ctx.enter_context(tc.tile_pool(name="line", bufs=2 * GROUP_HEADS))
         rope_pool = ctx.enter_context(tc.tile_pool(name="rope", bufs=3))
         turn_psum = ctx.enter_context(tc.psum_pool(name="turn_psum", bufs=4))
         acc_psum = ctx.enter_context(tc.psum_pool(name="acc_psum", bufs=4))
@@ -229,9 +230,9 @@ def tile_stickyllamaattention_pa_kernel(tc, hidden_states, wq, wk, out_0, out_1)
         def prepare(i):
             kind, a, b = units[i]
             words = raw_tiles[i][:].bitcast(F32)
-            if kind == "x":
-                grouped = x_stage.tile([P, PASSES, 4 * P], BF16, name="x_grouped", align_bytes=64)
-                dest = grouped[:].bitcast(F32).rearrange("p g (r u) -> p g r u", u=2)
+            if kind != "w":
+                grouped = stage.tile([P, 4, 4 * P], BF16, name="grouped", align_bytes=64)
+                dest = grouped[:].bitcast(F32).rearrange("p a (r u) -> p a r u", u=2)
             else:
                 if b == 0:
                     w_grouped[a] = w_stage.tile([P, PASSES, 4 * 512], BF16, name="w_grouped", align_bytes=64)
@@ -240,8 +241,11 @@ def tile_stickyllamaattention_pa_kernel(tc, hidden_states, wq, wk, out_0, out_1)
             for bank in range(PASSES // 2):
                 turned = turn_psum.tile([P, 4, P], F32, name="turned")
                 for slot in range(4):
-                    g, u = 2 * bank + slot // 2, slot % 2
-                    source = lined_tiles[i][:, g, u, :] if lined_up(i) else words[:, 256 * g + u : 256 * (g + 1) : 2]
+                    part, u = 2 * bank + slot // 2, slot % 2
+                    if kind == "g":
+                        source = lined_tiles[i - b + part][:, b, u, :]
+                    else:
+                        source = words[:, 256 * part + u : 256 * (part + 1) : 2]
                     nc.tensor.transpose(out=turned[:, slot, :], in_=source, identity=ident[:])
                 nc.scalar.copy(
                     out=dest[:, 2 * bank : 2 * bank + 2],
@@ -252,6 +256,12 @@ def tile_stickyllamaattention_pa_kernel(tc, hidden_states, wq, wk, out_0, out_1)
                     out=x_codes[a][:].rearrange("p g r -> p (g r)").bitcast(E5M2X4),
                     scales=x_scales[a][:].rearrange("p g r -> p (g r)"),
                     in_=grouped[:].rearrange("p g c -> p (g c)"),
+                )
+            elif kind == "g":
+                nc.vector.quantize_mx(
+                    out=w_codes[a][:, b, :].bitcast(E5M2X4),
+                    scales=w_scales[a][:, b, :],
+                    in_=grouped[:].rearrange("p h c -> p (h c)"),
                 )
             elif b == GROUP_HEADS - 1:
                 for g in range(0, PASSES, 2):
@@ -267,9 +277,8 @@ def tile_stickyllamaattention_pa_kernel(tc, hidden_states, wq, wk, out_0, out_1)
                 prepare(i)
                 if i < HEAD_UNITS:
                     idle_matmuls(KEEP_WARM)
-            for i in range(first + count, first + count + LINE_AHEAD):
-                if i not in lined_tiles:
-                    line_up(i)
+            for i in range(first + LINE_AHEAD, first + count + LINE_AHEAD):
+                line_up(i)
 
         pair = {}
 
@@ -297,13 +306,9 @@ def tile_stickyllamaattention_pa_kernel(tc, hidden_states, wq, wk, out_0, out_1)
             )
             view = q_view[:, GROUP_HEADS * n : GROUP_HEADS * (n + 1)] if n < GROUPS - 1 else k_view
             if n == GROUPS - 1 and t >= TOKEN_TILES - 2:
-                for lo in (0, HALF):
-                    nc.vector.tensor_tensor(
-                        out=prod[:, 0, :, e, lo : lo + HALF],
-                        in0=prod[:, 0, :, e, lo : lo + HALF],
-                        in1=prod[:, 1, :, e, HALF - lo : D - lo],
-                        op=ALU.add,
-                    )
+                by_cos = prod[:, 0, :, e, :].rearrange("p h (a j) -> p h a j", a=2)
+                by_sin = prod[:, 1, :, e, :].rearrange("p h (a j) -> p h a j", a=2)
+                nc.vector.tensor_tensor(out=by_cos, in0=by_cos, in1=by_sin[:, :, ::-1, :], op=ALU.add)
                 nc.scalar.dma_start(out=view[:, :, t * D : (t + 1) * D], in_=prod[:, 0, :, e, :])
             elif e == 1:
                 by_cos = prod[:, 0].rearrange("p h e (a j) -> p (h e) a j", a=2)

@@ -175,7 +175,7 @@ def tile_stickyllamaattention_pa_kernel(tc, hidden_states, wq, wk, out_0, out_1)
         stage = ctx.enter_context(tc.tile_pool(name="stage", bufs=3))
         w_stage = ctx.enter_context(tc.tile_pool(name="w_stage", bufs=1))
         line_pool = ctx.enter_context(tc.tile_pool(name="line", bufs=2 * GROUP_HEADS))
-        rope_pool = ctx.enter_context(tc.tile_pool(name="rope", bufs=3))
+        rope_pool = ctx.enter_context(tc.tile_pool(name="rope", bufs=4))
         turn_psum = ctx.enter_context(tc.psum_pool(name="turn_psum", bufs=4))
         acc_psum = ctx.enter_context(tc.psum_pool(name="acc_psum", bufs=4))
         ctx.enter_context(tc.manual_schedule())

@@ -305,11 +305,14 @@ def tile_stickyllamaattention_pa_kernel(tc, hidden_states, wq, wk, out_0, out_1)
                 op=ALU.mult,
             )
             view = q_view[:, GROUP_HEADS * n : GROUP_HEADS * (n + 1)] if n < GROUPS - 1 else k_view
-            if n == GROUPS - 1 and t >= TOKEN_TILES - 2:
-                by_cos = prod[:, 0, :, e, :].rearrange("p h (a j) -> p h a j", a=2)
-                by_sin = prod[:, 1, :, e, :].rearrange("p h (a j) -> p h a j", a=2)
-                nc.vector.tensor_tensor(out=by_cos, in0=by_cos, in1=by_sin[:, :, ::-1, :], op=ALU.add)
-                nc.scalar.dma_start(out=view[:, :, t * D : (t + 1) * D], in_=prod[:, 0, :, e, :])
+            if n == GROUPS - 1 and t == TOKEN_TILES - 2:
+                pass
+            elif n == GROUPS - 1 and t == TOKEN_TILES - 1:
+                for f in range(2):
+                    by_cos = prod[:, 0, :, f, :].rearrange("p h (a j) -> p h a j", a=2)
+                    by_sin = prod[:, 1, :, f, :].rearrange("p h (a j) -> p h a j", a=2)
+                    nc.vector.tensor_tensor(out=by_cos, in0=by_cos, in1=by_sin[:, :, ::-1, :], op=ALU.add)
+                    nc.scalar.dma_start(out=view[:, :, (t - 1 + f) * D : (t + f) * D], in_=prod[:, 0, :, f, :])
             elif e == 1:
                 by_cos = prod[:, 0].rearrange("p h e (a j) -> p (h e) a j", a=2)
                 by_sin = prod[:, 1].rearrange("p h e (a j) -> p (h e) a j", a=2)

@@ -31,7 +31,7 @@ RAW_BUFS = 12
 HEAD_UNITS = 6
 EARLY_UNITS = 16
 LATE_FIRST_PRODUCT = 7
-WARM_UP = 8
+WARM_UP = 5
 KEEP_WARM = 2
 LINE_AHEAD = 4
 

@@ -31,8 +31,8 @@ RAW_BUFS = 12
 HEAD_UNITS = 6
 EARLY_UNITS = 16
 LATE_FIRST_PRODUCT = 7
-WARM_UP = 5
 KEEP_WARM = 2
+SINES_ON_VECTOR = True
 LINE_AHEAD = 4
 
 
@@ -117,13 +117,15 @@ def reduced_angles(nc, work):
     return rest
 
 
-def rope_tables(nc, keep, work, rest):
+def half_sines(nc, work, rest):
     sin_half = scratch(work, "b", "sin_half")
     nc.scalar.activation(out=flat(sin_half), in_=flat(rest), func=ACT.Sin, scale=0.5)
     sin_quarter = scratch(work, "c", "sin_quarter")
     nc.scalar.activation(out=flat(sin_quarter), in_=flat(rest), func=ACT.Sin, scale=0.25)
+    return sin_half, sin_quarter
 
-    cos_sin = keep.tile([P, TOKEN_TILES, 2, D], F32, name="cos_sin")
+
+def cosines(nc, work, cos_sin, sin_half):
     square_half = scratch(work, "d", "square_half")
     nc.vector.tensor_tensor(out=square_half[:], in0=sin_half[:], in1=sin_half[:], op=ALU.mult)
     for lo in (0, HALF):
@@ -135,16 +137,19 @@ def rope_tables(nc, keep, work, rest):
             op0=ALU.mult,
             op1=ALU.add,
         )
+
+
+def sines_of(nc, work, cos_sin, sin_half, sin_quarter):
+    sines = nc.vector if SINES_ON_VECTOR else nc.gpsimd
     two_cos_half = scratch(work, "a", "two_cos_half")
-    nc.gpsimd.tensor_tensor(out=two_cos_half[:], in0=sin_quarter[:], in1=sin_quarter[:], op=ALU.mult)
-    nc.gpsimd.tensor_scalar(
+    sines.tensor_tensor(out=two_cos_half[:], in0=sin_quarter[:], in1=sin_quarter[:], op=ALU.mult)
+    sines.tensor_scalar(
         out=two_cos_half[:], in0=two_cos_half[:], scalar1=-4.0, scalar2=2.0, op0=ALU.mult, op1=ALU.add
     )
-    nc.gpsimd.tensor_tensor(out=cos_sin[:, :, 1, 0:HALF], in0=sin_half[:], in1=two_cos_half[:], op=ALU.mult)
-    nc.gpsimd.tensor_scalar(
+    sines.tensor_tensor(out=cos_sin[:, :, 1, 0:HALF], in0=sin_half[:], in1=two_cos_half[:], op=ALU.mult)
+    sines.tensor_scalar(
         out=cos_sin[:, :, 1, HALF:D], in0=cos_sin[:, :, 1, 0:HALF], scalar1=-1.0, scalar2=0.0, op0=ALU.mult, op1=ALU.add
     )
-    return cos_sin
 
 
 def tile_stickyllamaattention_pa_kernel(tc, hidden_states, wq, wk, out_0, out_1):
@@ -191,6 +196,15 @@ def tile_stickyllamaattention_pa_kernel(tc, hidden_states, wq, wk, out_0, out_1)
         for i in range(RAW_BUFS):
             load(i)
 
+        zero = work.tile([P, 1], F32, name="zero")
+        nc.vector.memset(zero[:], 0.0)
+        warm = work.tile([P, 1], F32, name="warm")
+        nc.scalar.activation(out=warm[:], in_=zero[:], func=ACT.Sin)
+
+        rest = reduced_angles(nc, work)
+        ident = keep.tile([P, P], F32, name="ident")
+        make_identity(nc, ident[:])
+
         idle = keep.tile([P, 512], BF16, name="idle")
         nc.gpsimd.memset(idle[:], 0.0)
         spin = acc_psum.tile([P, GROUP_HEADS, D], F32, name="acc")
@@ -200,17 +214,6 @@ def tile_stickyllamaattention_pa_kernel(tc, hidden_states, wq, wk, out_0, out_1)
                 nc.tensor.matmul(
                     out=spin[:].rearrange("p h d -> p (h d)"), lhsT=idle[:, 0:P], rhs=idle[:], start=True, stop=True
                 )
-
-        idle_matmuls(WARM_UP)
-
-        zero = work.tile([P, 1], F32, name="zero")
-        nc.vector.memset(zero[:], 0.0)
-        warm = work.tile([P, 1], F32, name="warm")
-        nc.scalar.activation(out=warm[:], in_=zero[:], func=ACT.Sin)
-
-        rest = reduced_angles(nc, work)
-        ident = keep.tile([P, P], F32, name="ident")
-        make_identity(nc, ident[:])
 
         x_codes = [keep.tile([P, PASSES, P], U32, name="x_codes%d" % t, align_bytes=64) for t in range(TOKEN_TILES)]
         x_scales = [keep.tile([P, PASSES, P], U8, name="x_scales%d" % t, align_bytes=64) for t in range(TOKEN_TILES)]
@@ -227,7 +230,9 @@ def tile_stickyllamaattention_pa_kernel(tc, hidden_states, wq, wk, out_0, out_1)
                 )
                 lined_tiles[i] = lined
 
-        def prepare(i):
+        staged = {}
+
+        def turn(i):
             kind, a, b = units[i]
             words = raw_tiles[i][:].bitcast(F32)
             if kind != "w":
@@ -251,6 +256,17 @@ def tile_stickyllamaattention_pa_kernel(tc, hidden_states, wq, wk, out_0, out_1)
                     out=dest[:, 2 * bank : 2 * bank + 2],
                     in_=turned[:].rearrange("p (g u) r -> p g r u", u=2),
                 )
+            staged[i] = grouped
+            load(i + RAW_BUFS)
+
+        def quantise_first_group(g):
+            nc.vector.quantize_mx(
+                out=w_codes[0][:, g, :].bitcast(E5M2X4), scales=w_scales[0][:, g, :], in_=w_grouped[0][:, g, :]
+            )
+
+        def quantise(i):
+            kind, a, b = units[i]
+            grouped = staged[i]
             if kind == "x":
                 nc.vector.quantize_mx(
                     out=x_codes[a][:].rearrange("p g r -> p (g r)").bitcast(E5M2X4),
@@ -270,20 +286,21 @@ def tile_stickyllamaattention_pa_kernel(tc, hidden_states, wq, wk, out_0, out_1)
                         scales=w_scales[a][:, g : g + 2, :].rearrange("p g c -> p (g c)"),
                         in_=grouped[:, g : g + 2, :].rearrange("p g c -> p (g c)"),
                     )
-            load(i + RAW_BUFS)
 
         def prepare_run(first, count):
             for i in range(first, first + count):
-                prepare(i)
-                if i < HEAD_UNITS:
-                    idle_matmuls(KEEP_WARM)
+                turn(i)
+                quantise(i)
             for i in range(first + LINE_AHEAD, first + count + LINE_AHEAD):
                 line_up(i)
 
         pair = {}
 
-        def product(n, t):
+        sums = {}
+
+        def multiply(n, t):
             acc = acc_psum.tile([P, GROUP_HEADS, D], F32, name="acc")
+            sums[(n, t)] = acc
             for g in range(PASSES):
                 nc.tensor.matmul_mx(
                     out=acc[:].rearrange("p h d -> p (h d)"),
@@ -294,6 +311,9 @@ def tile_stickyllamaattention_pa_kernel(tc, hidden_states, wq, wk, out_0, out_1)
                     start=(g == 0),
                     stop=(g == PASSES - 1),
                 )
+
+        def rotate(n, t):
+            acc = sums[(n, t)]
             e = t % 2
             if e == 0:
                 pair["prod"] = rope_pool.tile([P, 2, GROUP_HEADS, 2, D], F32, name="prod")
@@ -301,7 +321,7 @@ def tile_stickyllamaattention_pa_kernel(tc, hidden_states, wq, wk, out_0, out_1)
             nc.vector.tensor_tensor(
                 out=prod[:, :, :, e, :],
                 in0=acc[:].unsqueeze(1).to_broadcast([P, 2, GROUP_HEADS, D]),
-                in1=tables["cos_sin"][:, t].unsqueeze(2).to_broadcast([P, 2, GROUP_HEADS, D]),
+                in1=cos_sin[:, t].unsqueeze(2).to_broadcast([P, 2, GROUP_HEADS, D]),
                 op=ALU.mult,
             )
             view = q_view[:, GROUP_HEADS * n : GROUP_HEADS * (n + 1)] if n < GROUPS - 1 else k_view
@@ -321,13 +341,30 @@ def tile_stickyllamaattention_pa_kernel(tc, hidden_states, wq, wk, out_0, out_1)
                     out=view[:, :, (t - 1) * D : (t + 1) * D], in_=prod[:, 0].rearrange("p h e d -> p h (e d)")
                 )
 
-        tables = {}
-        prepare_run(0, 2)
-        tables["cos_sin"] = rope_tables(nc, keep, work, rest)
-        prepare_run(2, HEAD_UNITS - 2)
-        done = HEAD_UNITS
-        for number in range(GROUPS * TOKEN_TILES):
-            product(number // TOKEN_TILES, number % TOKEN_TILES)
+        cos_sin = keep.tile([P, TOKEN_TILES, 2, D], F32, name="cos_sin")
+        for i in range(5):
+            turn(i)
+        quantise_first_group(0)
+        quantise_first_group(1)
+        quantise(4)
+        quantise_first_group(2)
+        quantise_first_group(3)
+        sin_half, sin_quarter = half_sines(nc, work, rest)
+        turn(5)
+        idle_matmuls(KEEP_WARM)
+        quantise(5)
+        multiply(0, 0)
+        turn(6)
+        turn(7)
+        cosines(nc, work, cos_sin, sin_half)
+        quantise(6)
+        quantise(7)
+        sines_of(nc, work, cos_sin, sin_half, sin_quarter)
+        rotate(0, 0)
+        done = HEAD_UNITS + 2
+        for number in range(1, GROUPS * TOKEN_TILES):
+            multiply(number // TOKEN_TILES, number % TOKEN_TILES)
+            rotate(number // TOKEN_TILES, number % TOKEN_TILES)
             if done < EARLY_UNITS:
                 count = 2
             elif done < len(units) and number >= LATE_FIRST_PRODUCT and (number - LATE_FIRST_PRODUCT) % 2 == 0:

@@ -32,6 +32,7 @@ HEAD_UNITS = 6
 EARLY_UNITS = 16
 LATE_FIRST_PRODUCT = 7
 KEEP_WARM = 2
+VECTOR_ADDS = (1,)
 SINES_ON_VECTOR = True
 LINE_AHEAD = 4
 
@@ -177,7 +178,7 @@ def tile_stickyllamaattention_pa_kernel(tc, hidden_states, wq, wk, out_0, out_1)
         keep = ctx.enter_context(tc.tile_pool(name="keep", bufs=1))
         work = ctx.enter_context(tc.tile_pool(name="work", bufs=1))
         raw_pool = ctx.enter_context(tc.tile_pool(name="raw", bufs=RAW_BUFS))
-        stage = ctx.enter_context(tc.tile_pool(name="stage", bufs=3))
+        stage = ctx.enter_context(tc.tile_pool(name="stage", bufs=5))
         w_stage = ctx.enter_context(tc.tile_pool(name="w_stage", bufs=1))
         line_pool = ctx.enter_context(tc.tile_pool(name="line", bufs=2 * GROUP_HEADS))
         rope_pool = ctx.enter_context(tc.tile_pool(name="rope", bufs=4))
@@ -336,7 +337,8 @@ def tile_stickyllamaattention_pa_kernel(tc, hidden_states, wq, wk, out_0, out_1)
             elif e == 1:
                 by_cos = prod[:, 0].rearrange("p h e (a j) -> p (h e) a j", a=2)
                 by_sin = prod[:, 1].rearrange("p h e (a j) -> p (h e) a j", a=2)
-                nc.gpsimd.tensor_tensor(out=by_cos, in0=by_cos, in1=by_sin[:, :, ::-1, :], op=ALU.add)
+                adder = nc.vector if TOKEN_TILES * n + t in VECTOR_ADDS else nc.gpsimd
+                adder.tensor_tensor(out=by_cos, in0=by_cos, in1=by_sin[:, :, ::-1, :], op=ALU.add)
                 nc.sync.dma_start(
                     out=view[:, :, (t - 1) * D : (t + 1) * D], in_=prod[:, 0].rearrange("p h e d -> p h (e d)")
                 )

@@ -353,10 +353,10 @@ def tile_stickyllamaattention_pa_kernel(tc, hidden_states, wq, wk, out_0, out_1)
         quantise_first_group(3)
         sin_half, sin_quarter = half_sines(nc, work, rest)
         turn(5)
+        turn(6)
         idle_matmuls(KEEP_WARM)
         quantise(5)
         multiply(0, 0)
-        turn(6)
         turn(7)
         cosines(nc, work, cos_sin, sin_half)
         quantise(6)

@@ -299,10 +299,11 @@ def tile_stickyllamaattention_pa_kernel(tc, hidden_states, wq, wk, out_0, out_1)
 
         sums = {}
 
-        def multiply(n, t):
-            acc = acc_psum.tile([P, GROUP_HEADS, D], F32, name="acc")
-            sums[(n, t)] = acc
-            for g in range(PASSES):
+        def multiply(n, t, passes=range(PASSES)):
+            if passes[0] == 0:
+                sums[(n, t)] = acc_psum.tile([P, GROUP_HEADS, D], F32, name="acc")
+            acc = sums[(n, t)]
+            for g in passes:
                 nc.tensor.matmul_mx(
                     out=acc[:].rearrange("p h d -> p (h d)"),
                     lhsT=x_codes[t][:, g, :].bitcast(E5M2X4),
@@ -365,6 +366,18 @@ def tile_stickyllamaattention_pa_kernel(tc, hidden_states, wq, wk, out_0, out_1)
         rotate(0, 0)
         done = HEAD_UNITS + 2
         for number in range(1, GROUPS * TOKEN_TILES):
+            if done < EARLY_UNITS:
+                multiply(number // TOKEN_TILES, number % TOKEN_TILES, range(0, 2))
+                turn(done)
+                multiply(number // TOKEN_TILES, number % TOKEN_TILES, range(2, PASSES))
+                turn(done + 1)
+                rotate(number // TOKEN_TILES, number % TOKEN_TILES)
+                quantise(done)
+                quantise(done + 1)
+                for i in range(done + LINE_AHEAD, done + 2 + LINE_AHEAD):
+                    line_up(i)
+                done += 2
+                continue
             multiply(number // TOKEN_TILES, number % TOKEN_TILES)
             rotate(number // TOKEN_TILES, number % TOKEN_TILES)
             if done < EARLY_UNITS:

from contextlib import ExitStack

import concourse.mybir as mybir
from concourse.masks import make_identity

S, K, D = 1024, 2048, 128
Q_HEADS, KV_HEADS = 16, 4
ROPE_BASE, ROPE_FACTOR, ORIG_MAX_POS = 5.0e5, 8.0, 8192
LOW_FREQ, HIGH_FREQ = 1.0, 4.0

FLOPS = 2 * S * (Q_HEADS + KV_HEADS) * D * K

F32 = mybir.dt.float32
BF16 = mybir.dt.bfloat16
I32 = mybir.dt.int32
U32 = mybir.dt.uint32
U8 = mybir.dt.uint8
E5M2X4 = mybir.dt.float8_e5m2_x4
ALU = mybir.AluOpType
ACT = mybir.ActivationFunctionType

PI = 3.141592653589793
P = 128
HALF = D // 2
PASSES = K // 512
TOKEN_TILES = S // P
GROUP_HEADS = 4
GROUPS = (Q_HEADS + KV_HEADS) // GROUP_HEADS
RAW_BUFS = 12

HEAD_UNITS = 6
EARLY_UNITS = 16
LATE_FIRST_PRODUCT = 7
KEEP_WARM = 2
VECTOR_ADDS = (1,)
SINES_ON_VECTOR = True
LINE_AHEAD = 4


def lined_up(i):
    return i >= EARLY_UNITS


TWO_PI_HI = 6.28125
TWO_PI_LO = 2.0 * PI - TWO_PI_HI


def rope_smooth(j):
    inv_freq = ROPE_BASE ** (-2.0 * j / D)
    ratio = ORIG_MAX_POS * inv_freq / (2.0 * PI)
    return min(max((ratio - LOW_FREQ) / (HIGH_FREQ - LOW_FREQ), 0.0), 1.0)


def rope_freq(j):
    inv_freq = ROPE_BASE ** (-2.0 * j / D)
    smooth = rope_smooth(j)
    return (1.0 - smooth) * inv_freq / ROPE_FACTOR + smooth * inv_freq


def scratch(work, slot, name, dtype=F32):
    return work.tile([P, TOKEN_TILES, HALF], dtype, name=name, tag="scratch_" + slot)


def flat(tile_ap):
    return tile_ap[:].rearrange("p t j -> p (t j)")


def reduced_angles(nc, work):
    tpos = work.tile([P, TOKEN_TILES, 1], F32, name="tpos")
    nc.gpsimd.iota(
        tpos[:].rearrange("p t o -> p (t o)"),
        pattern=[[1, TOKEN_TILES]],
        base=0,
        channel_multiplier=TOKEN_TILES,
        allow_small_or_imprecise_dtypes=True,
    )

    angle = scratch(work, "a", "angle")
    nc.vector.tensor_copy(out=angle[:, :, 0:1], in_=tpos[:])
    for level in range(6):
        w = 2**level
        nc.vector.tensor_scalar(
            out=angle[:, :, w : 2 * w],
            in0=angle[:, :, 0:w],
            scalar1=ROPE_BASE ** (-2.0 * w / D),
            scalar2=None,
            op0=ALU.mult,
        )
    divided = [j for j in range(HALF) if rope_smooth(j) == 0.0]
    assert divided == list(range(divided[0], HALF))
    nc.vector.tensor_scalar(
        out=angle[:, :, divided[0] :],
        in0=angle[:, :, divided[0] :],
        scalar1=1.0 / ROPE_FACTOR,
        scalar2=None,
        op0=ALU.mult,
    )
    for j in range(HALF):
        if 0.0 < rope_smooth(j) < 1.0:
            nc.vector.tensor_scalar(
                out=angle[:, :, j : j + 1], in0=tpos[:], scalar1=rope_freq(j), scalar2=None, op0=ALU.mult
            )

    turns_int = scratch(work, "b", "turns_int", I32)
    nc.vector.tensor_scalar(
        out=flat(turns_int), in0=flat(angle), scalar1=1.0 / (2.0 * PI), scalar2=0.25, op0=ALU.mult, op1=ALU.add
    )
    turns = scratch(work, "c", "turns")
    nc.vector.tensor_copy(out=flat(turns), in_=flat(turns_int))
    rest_hi = scratch(work, "d", "rest_hi")
    nc.vector.scalar_tensor_tensor(
        out=flat(rest_hi), in0=flat(turns), scalar=-TWO_PI_HI, in1=flat(angle), op0=ALU.mult, op1=ALU.add
    )
    rest = scratch(work, "a", "rest")
    nc.vector.scalar_tensor_tensor(
        out=flat(rest), in0=flat(turns), scalar=-TWO_PI_LO, in1=flat(rest_hi), op0=ALU.mult, op1=ALU.add
    )
    return rest


def half_sines(nc, work, rest):
    sin_half = scratch(work, "b", "sin_half")
    nc.scalar.activation(out=flat(sin_half), in_=flat(rest), func=ACT.Sin, scale=0.5)
    sin_quarter = scratch(work, "c", "sin_quarter")
    nc.scalar.activation(out=flat(sin_quarter), in_=flat(rest), func=ACT.Sin, scale=0.25)
    return sin_half, sin_quarter


def cosines(nc, work, cos_sin, sin_half):
    square_half = scratch(work, "d", "square_half")
    nc.vector.tensor_tensor(out=square_half[:], in0=sin_half[:], in1=sin_half[:], op=ALU.mult)
    for lo in (0, HALF):
        nc.vector.tensor_scalar(
            out=cos_sin[:, :, 0, lo : lo + HALF],
            in0=square_half[:],
            scalar1=-2.0,
            scalar2=1.0,
            op0=ALU.mult,
            op1=ALU.add,
        )


def sines_of(nc, work, cos_sin, sin_half, sin_quarter):
    sines = nc.vector if SINES_ON_VECTOR else nc.gpsimd
    two_cos_half = scratch(work, "a", "two_cos_half")
    sines.tensor_tensor(out=two_cos_half[:], in0=sin_quarter[:], in1=sin_quarter[:], op=ALU.mult)
    sines.tensor_scalar(
        out=two_cos_half[:], in0=two_cos_half[:], scalar1=-4.0, scalar2=2.0, op0=ALU.mult, op1=ALU.add
    )
    sines.tensor_tensor(out=cos_sin[:, :, 1, 0:HALF], in0=sin_half[:], in1=two_cos_half[:], op=ALU.mult)
    sines.tensor_scalar(
        out=cos_sin[:, :, 1, HALF:D], in0=cos_sin[:, :, 1, 0:HALF], scalar1=-1.0, scalar2=0.0, op0=ALU.mult, op1=ALU.add
    )


def tile_stickyllamaattention_pa_kernel(tc, hidden_states, wq, wk, out_0, out_1):
    nc = tc.nc

    x_rows = hidden_states[0].rearrange("(p e) k -> e p k", e=TOKEN_TILES)
    units = [("w", 0, h) for h in range(GROUP_HEADS)]
    units += [("x", t, 0) for t in range(TOKEN_TILES)]
    units += [("w", 1, h) for h in range(GROUP_HEADS)]
    units += [("g", n, b) for n in range(2, GROUPS) for b in range(GROUP_HEADS)]

    def unit_rows(unit):
        kind, a, b = unit
        if kind == "x":
            return x_rows[a]
        head = GROUP_HEADS * a + b
        if head < Q_HEADS:
            return wq[head * D : (head + 1) * D, :]
        return wk[(head - Q_HEADS) * D : (head - Q_HEADS + 1) * D, :]

    q_view = out_0[0].rearrange("h (p e) d -> p h (e d)", e=TOKEN_TILES)
    k_view = out_1[0].rearrange("h (p e) d -> p h (e d)", e=TOKEN_TILES)

    with ExitStack() as ctx:
        keep = ctx.enter_context(tc.tile_pool(name="keep", bufs=1))
        work = ctx.enter_context(tc.tile_pool(name="work", bufs=1))
        raw_pool = ctx.enter_context(tc.tile_pool(name="raw", bufs=RAW_BUFS))
        stage = ctx.enter_context(tc.tile_pool(name="stage", bufs=5))
        w_stage = ctx.enter_context(tc.tile_pool(name="w_stage", bufs=1))
        line_pool = ctx.enter_context(tc.tile_pool(name="line", bufs=2 * GROUP_HEADS))
        rope_pool = ctx.enter_context(tc.tile_pool(name="rope", bufs=4))
        turn_psum = ctx.enter_context(tc.psum_pool(name="turn_psum", bufs=4))
        acc_psum = ctx.enter_context(tc.psum_pool(name="acc_psum", bufs=4))
        ctx.enter_context(tc.manual_schedule())

        raw_tiles = {}

        def load(i):
            if i < len(units):
                raw = raw_pool.tile([P, K], BF16, name="raw")
                nc.sync.dma_start(out=raw[:], in_=unit_rows(units[i]))
                raw_tiles[i] = raw

        for i in range(RAW_BUFS):
            load(i)

        zero = work.tile([P, 1], F32, name="zero")
        nc.vector.memset(zero[:], 0.0)
        warm = work.tile([P, 1], F32, name="warm")
        nc.scalar.activation(out=warm[:], in_=zero[:], func=ACT.Sin)

        rest = reduced_angles(nc, work)
        ident = keep.tile([P, P], F32, name="ident")
        make_identity(nc, ident[:])

        idle = keep.tile([P, 512], BF16, name="idle")
        nc.gpsimd.memset(idle[:], 0.0)
        spin = acc_psum.tile([P, GROUP_HEADS, D], F32, name="acc")

        def idle_matmuls(count):
            for k in range(count):
                nc.tensor.matmul(
                    out=spin[:].rearrange("p h d -> p (h d)"), lhsT=idle[:, 0:P], rhs=idle[:], start=True, stop=True
                )

        x_codes = [keep.tile([P, PASSES, P], U32, name="x_codes%d" % t, align_bytes=64) for t in range(TOKEN_TILES)]
        x_scales = [keep.tile([P, PASSES, P], U8, name="x_scales%d" % t, align_bytes=64) for t in range(TOKEN_TILES)]
        w_codes = [keep.tile([P, PASSES, 512], U32, name="w_codes%d" % n, align_bytes=64) for n in range(GROUPS)]
        w_scales = [keep.tile([P, PASSES, 512], U8, name="w_scales%d" % n, align_bytes=64) for n in range(GROUPS)]
        w_grouped = {}
        lined_tiles = {}

        def line_up(i):
            if i < len(units) and lined_up(i):
                lined = line_pool.tile([P, PASSES, 2, P], F32, name="lined")
                nc.scalar.copy(
                    out=lined[:], in_=raw_tiles[i][:].bitcast(F32).rearrange("p (g w u) -> p g u w", g=PASSES, u=2)
                )
                lined_tiles[i] = lined

        staged = {}

        def turn(i):
            kind, a, b = units[i]
            words = raw_tiles[i][:].bitcast(F32)
            if kind != "w":
                grouped = stage.tile([P, 4, 4 * P], BF16, name="grouped", align_bytes=64)
                dest = grouped[:].bitcast(F32).rearrange("p a (r u) -> p a r u", u=2)
            else:
                if b == 0:
                    w_grouped[a] = w_stage.tile([P, PASSES, 4 * 512], BF16, name="w_grouped", align_bytes=64)
                grouped = w_grouped[a]
                dest = grouped[:].bitcast(F32).rearrange("p g (h r u) -> p g h r u", h=GROUP_HEADS, u=2)[:, :, b]
            for bank in range(PASSES // 2):
                turned = turn_psum.tile([P, 4, P], F32, name="turned")
                for slot in range(4):
                    part, u = 2 * bank + slot // 2, slot % 2
                    if kind == "g":
                        source = lined_tiles[i - b + part][:, b, u, :]
                    else:
                        source = words[:, 256 * part + u : 256 * (part + 1) : 2]
                    nc.tensor.transpose(out=turned[:, slot, :], in_=source, identity=ident[:])
                nc.scalar.copy(
                    out=dest[:, 2 * bank : 2 * bank + 2],
                    in_=turned[:].rearrange("p (g u) r -> p g r u", u=2),
                )
            staged[i] = grouped
            load(i + RAW_BUFS)

        def quantise_first_group(g):
            nc.vector.quantize_mx(
                out=w_codes[0][:, g, :].bitcast(E5M2X4), scales=w_scales[0][:, g, :], in_=w_grouped[0][:, g, :]
            )

        def quantise(i):
            kind, a, b = units[i]
            grouped = staged[i]
            if kind == "x":
                nc.vector.quantize_mx(
                    out=x_codes[a][:].rearrange("p g r -> p (g r)").bitcast(E5M2X4),
                    scales=x_scales[a][:].rearrange("p g r -> p (g r)"),
                    in_=grouped[:].rearrange("p g c -> p (g c)"),
                )
            elif kind == "g":
                nc.vector.quantize_mx(
                    out=w_codes[a][:, b, :].bitcast(E5M2X4),
                    scales=w_scales[a][:, b, :],
                    in_=grouped[:].rearrange("p h c -> p (h c)"),
                )
            elif b == GROUP_HEADS - 1:
                for g in range(0, PASSES, 2):
                    nc.vector.quantize_mx(
                        out=w_codes[a][:, g : g + 2, :].rearrange("p g c -> p (g c)").bitcast(E5M2X4),
                        scales=w_scales[a][:, g : g + 2, :].rearrange("p g c -> p (g c)"),
                        in_=grouped[:, g : g + 2, :].rearrange("p g c -> p (g c)"),
                    )

        def prepare_run(first, count):
            for i in range(first, first + count):
                turn(i)
                quantise(i)
            for i in range(first + LINE_AHEAD, first + count + LINE_AHEAD):
                line_up(i)

        pair = {}

        sums = {}

        def multiply(n, t, passes=range(PASSES)):
            if passes[0] == 0:
                sums[(n, t)] = acc_psum.tile([P, GROUP_HEADS, D], F32, name="acc")
            acc = sums[(n, t)]
            for g in passes:
                nc.tensor.matmul_mx(
                    out=acc[:].rearrange("p h d -> p (h d)"),
                    lhsT=x_codes[t][:, g, :].bitcast(E5M2X4),
                    lhsT_scale=x_scales[t][:, g, :],
                    rhs=w_codes[n][:, g, :].bitcast(E5M2X4),
                    rhs_scale=w_scales[n][:, g, :],
                    start=(g == 0),
                    stop=(g == PASSES - 1),
                )

        def rotate(n, t):
            acc = sums[(n, t)]
            e = t % 2
            if e == 0:
                pair["prod"] = rope_pool.tile([P, 2, GROUP_HEADS, 2, D], F32, name="prod")
            prod = pair["prod"]
            nc.vector.tensor_tensor(
                out=prod[:, :, :, e, :],
                in0=acc[:].unsqueeze(1).to_broadcast([P, 2, GROUP_HEADS, D]),
                in1=cos_sin[:, t].unsqueeze(2).to_broadcast([P, 2, GROUP_HEADS, D]),
                op=ALU.mult,
            )
            view = q_view[:, GROUP_HEADS * n : GROUP_HEADS * (n + 1)] if n < GROUPS - 1 else k_view
            if n == GROUPS - 1 and t == TOKEN_TILES - 2:
                pass
            elif n == GROUPS - 1 and t == TOKEN_TILES - 1:
                for f in range(2):
                    by_cos = prod[:, 0, :, f, :].rearrange("p h (a j) -> p h a j", a=2)
                    by_sin = prod[:, 1, :, f, :].rearrange("p h (a j) -> p h a j", a=2)
                    nc.vector.tensor_tensor(out=by_cos, in0=by_cos, in1=by_sin[:, :, ::-1, :], op=ALU.add)
                    nc.scalar.dma_start(out=view[:, :, (t - 1 + f) * D : (t + f) * D], in_=prod[:, 0, :, f, :])
            elif e == 1:
                by_cos = prod[:, 0].rearrange("p h e (a j) -> p (h e) a j", a=2)
                by_sin = prod[:, 1].rearrange("p h e (a j) -> p (h e) a j", a=2)
                adder = nc.vector if TOKEN_TILES * n + t in VECTOR_ADDS else nc.gpsimd
                adder.tensor_tensor(out=by_cos, in0=by_cos, in1=by_sin[:, :, ::-1, :], op=ALU.add)
                nc.sync.dma_start(
                    out=view[:, :, (t - 1) * D : (t + 1) * D], in_=prod[:, 0].rearrange("p h e d -> p h (e d)")
                )

        cos_sin = keep.tile([P, TOKEN_TILES, 2, D], F32, name="cos_sin")
        for i in range(5):
            turn(i)
        quantise_first_group(0)
        quantise_first_group(1)
        quantise(4)
        quantise_first_group(2)
        quantise_first_group(3)
        sin_half, sin_quarter = half_sines(nc, work, rest)
        turn(5)
        turn(6)
        idle_matmuls(KEEP_WARM)
        quantise(5)
        multiply(0, 0)
        turn(7)
        cosines(nc, work, cos_sin, sin_half)
        quantise(6)
        quantise(7)
        sines_of(nc, work, cos_sin, sin_half, sin_quarter)
        rotate(0, 0)
        done = HEAD_UNITS + 2
        for number in range(1, GROUPS * TOKEN_TILES):
            if done < EARLY_UNITS:
                multiply(number // TOKEN_TILES, number % TOKEN_TILES, range(0, 2))
                turn(done)
                multiply(number // TOKEN_TILES, number % TOKEN_TILES, range(2, PASSES))
                turn(done + 1)
                rotate(number // TOKEN_TILES, number % TOKEN_TILES)
                quantise(done)
                quantise(done + 1)
                for i in range(done + LINE_AHEAD, done + 2 + LINE_AHEAD):
                    line_up(i)
                done += 2
                continue
            multiply(number // TOKEN_TILES, number % TOKEN_TILES)
            rotate(number // TOKEN_TILES, number % TOKEN_TILES)
            if done < EARLY_UNITS:
                count = 2
            elif done < len(units) and number >= LATE_FIRST_PRODUCT and (number - LATE_FIRST_PRODUCT) % 2 == 0:
                count = 1
            else:
                count = 0
            prepare_run(done, count)
            done += count
